import numpy as np
import ml_dtypes


def mxq(x, axis, fmt="e4m3"):
    dtype, down = {"e4m3": (ml_dtypes.float8_e4m3fn, 7), "e5m2": (ml_dtypes.float8_e5m2, 14)}[fmt]
    v = np.moveaxis(np.asarray(x, np.float32).astype(ml_dtypes.bfloat16).astype(np.float64), axis, -1)
    blocks = v.reshape(v.shape[:-1] + (-1, 32))
    amax = np.abs(blocks).max(-1, keepdims=True)
    byte = np.maximum(np.where(amax > 0, np.frexp(amax)[1] - 1 + 127, 0) - down, 1)
    scale = np.exp2(byte - 127.0)
    codes = (blocks / scale).astype(np.float32).astype(dtype).astype(np.float64)
    return np.moveaxis((codes * scale).reshape(v.shape), -1, axis)


BF16 = ml_dtypes.bfloat16


def bf(x):
    return np.asarray(x, np.float32).astype(BF16)


def f64(x):
    return np.asarray(x).astype(np.float64)


B, C, H, W = 64, 128, 32, 32
M = H * W


def setup_inputs():
    noise = np.random.standard_normal((B, C, H, W))
    shared = np.random.standard_normal((B, 1, H, W))
    gain = np.random.standard_normal((B, C, 1, 1))
    offset = np.random.standard_normal((B, C, 1, 1))
    return {"x": bf(noise + 0.7 * gain * shared + 0.5 * offset)}


def reference(x):
    xf = f64(x).reshape(B, C, M)
    xc = xf - np.mean(xf, axis=2, keepdims=True)
    xq = mxq(xc, 2, "e4m3")
    return (xq @ xq.transpose(0, 2, 1)) / M

@@ -1,0 +1,199 @@
+from contextlib import ExitStack
+
+import concourse.mybir as mybir
+from concourse.masks import make_identity
+
+FLOPS = 2 * 64 * 128 * 128 * 1024
+
+BF16 = mybir.dt.bfloat16
+F32 = mybir.dt.float32
+U32 = mybir.dt.uint32
+U8 = mybir.dt.uint8
+FP8X4 = mybir.dt.float8_e4m3fn_x4
+ALU = mybir.AluOpType
+ACT = mybir.ActivationFunctionType
+
+P = 128
+B = 64
+K = 1024
+HALF = 512
+GI = 4
+NG = B // GI
+UNITS = 2 * GI
+SCOL = 8
+
+
+def scalar_units(g):
+    n = 3 if g % 2 == 0 else 2
+    return list(range(UNITS - n, UNITS))
+
+
+def column_of(g, j):
+    su = scalar_units(g)
+    if j in su:
+        return SCOL + su.index(j)
+    return j
+
+
+def tile_covpool_kernel(tc, x, out):
+    nc = tc.nc
+    xv = x.rearrange("b c y z -> (b c y z)").rearrange("(s q j) -> q s j", s=2 * B, q=P, j=HALF)
+    ov = out.rearrange("b c n -> c b n")
+
+    with ExitStack() as ctx:
+        const = ctx.enter_context(tc.tile_pool(name="const", bufs=1))
+        xin = ctx.enter_context(tc.tile_pool(name="xin", bufs=1))
+        xcp = ctx.enter_context(tc.tile_pool(name="xcp", bufs=3))
+        grpp = ctx.enter_context(tc.tile_pool(name="grpp", bufs=3))
+        qp = ctx.enter_context(tc.tile_pool(name="qp", bufs=2))
+        outp = ctx.enter_context(tc.tile_pool(name="outp", bufs=4))
+        tpp = ctx.enter_context(tc.psum_pool(name="tpp", bufs=5))
+        accp = ctx.enter_context(tc.psum_pool(name="accp", bufs=2))
+        msp = ctx.enter_context(tc.psum_pool(name="msp", bufs=1))
+        ctx.enter_context(tc.manual_schedule())
+
+        xg = {}
+        xc = {}
+        grp = {}
+        codes = {}
+        scl = {}
+        acc = {}
+
+        for g in range(NG):
+            xg[g] = xin.tile([P, UNITS, HALF], BF16, name="x%d" % g, tag="x%d" % g)
+            pieces = 4 if g == 0 else (2 if g == 1 else 1)
+            step = UNITS // pieces
+            for a in range(0, UNITS, step):
+                nc.sync.dma_start(
+                    out=xg[g][:, a : a + step, :],
+                    in_=xv[:, UNITS * g + a : UNITS * g + a + step, :],
+                )
+
+        ident = const.tile([P, P], BF16, name="ident")
+        make_identity(nc, ident[:])
+        sums = const.tile([P, NG, 16], F32, name="sums")
+        nc.vector.memset(sums[:], 0.0)
+        negmean = const.tile([P, NG, 16], F32, name="negmean")
+        idv = ident[:].rearrange("p (a e) -> p a e", e=2)
+        pairs = const.tile([P, P // 2, 1], F32, name="pairs")
+        nc.vector.tensor_tensor(out=pairs[:], in0=idv[:, :, 0:1], in1=idv[:, :, 1:2], op=ALU.add)
+        gp = const.tile([P, P // 2, 2], F32, name="gp")
+        nc.vector.tensor_scalar(
+            out=gp[:],
+            in0=pairs[:].to_broadcast([P, P // 2, 2]),
+            scalar1=-1.0 / K,
+            scalar2=None,
+            op0=ALU.mult,
+        )
+        junk_v = const.tile([P, HALF], BF16, name="junk_v")
+        junk_s = const.tile([P, HALF], BF16, name="junk_s")
+
+        def sum_vector(g, j):
+            c = column_of(g, j)
+            nc.vector.tensor_scalar(
+                out=junk_v[:],
+                in0=xg[g][:, j, :],
+                scalar1=1.0,
+                scalar2=None,
+                op0=ALU.mult,
+                op1=ALU.add,
+                accum_out=sums[:, g, c : c + 1],
+            )
+
+        def sum_scalar(g, j):
+            c = column_of(g, j)
+            nc.scalar.activation(
+                out=junk_s[:], in_=xg[g][:, j, :], func=ACT.Copy, accum_out=sums[:, g, c : c + 1]
+            )
+
+        def mean(g):
+            ms = msp.tile([P, 16], F32, name="ms%d" % g, tag="ms")
+            nc.tensor.matmul(
+                out=ms[:],
+                lhsT=gp[:].rearrange("p a e -> p (a e)"),
+                rhs=sums[:, g, :],
+                start=True,
+                stop=True,
+            )
+            nc.scalar.copy(out=negmean[:, g, :], in_=ms[:])
+
+        def subtract(g):
+            xc[g] = xcp.tile([P, UNITS, HALF], BF16, name="xc%d" % g, tag="xc")
+            for j in range(UNITS):
+                c = column_of(g, j)
+                nc.vector.tensor_scalar(
+                    out=xc[g][:, j, :],
+                    in0=xg[g][:, j, :],
+                    scalar1=negmean[:, g, c : c + 1],
+                    scalar2=None,
+                    op0=ALU.add,
+                )
+
+        def transpose_and_copy(g):
+            grp[g] = grpp.tile([P, 2 * GI * HALF], BF16, name="grp%d" % g, tag="grp", align_bytes=64)
+            for i in range(GI):
+                tp = tpp.tile([P, 4, P, 2], BF16, name="tp%d_%d" % (g, i), tag="tp")
+                for h in range(2):
+                    for v in range(4):
+                        nc.tensor.transpose(
+                            out=tp[:, v, 64 * h : 64 * h + 64, :].rearrange("p a u -> p (a u)"),
+                            in_=xc[g][:, 2 * i + h, P * v : P * v + P],
+                            identity=ident[:],
+                        )
+                for a in range(2):
+                    off = (a * GI + i) * HALF
+                    nc.scalar.copy(
+                        out=grp[g][:, off : off + HALF].rearrange("p (c v u) -> p c v u", v=2, u=2),
+                        in_=tp[:, 2 * a : 2 * a + 2, :, :].rearrange("p v c u -> p c v u"),
+                    )
+
+        def quantise(g):
+            codes[g] = qp.tile([P, 2 * GI * P], U32, name="codes%d" % g, tag="codes", align_bytes=64)
+            scl[g] = qp.tile([P, 2 * GI * P], U8, name="scl%d" % g, tag="scl", align_bytes=64)
+            nc.vector.quantize_mx(out=codes[g][:].bitcast(FP8X4), scales=scl[g][:], in_=grp[g][:])
+
+        def multiply(g):
+            acc[g] = accp.tile([P, GI * P], F32, name="acc%d" % g, tag="acc")
+            for i in range(GI):
+                for a in range(2):
+                    off = (a * GI + i) * P
+                    nc.tensor.matmul_mx(
+                        out=acc[g][:, P * i : P * i + P],
+                        lhsT=codes[g][:, off : off + P].bitcast(FP8X4),
+                        lhsT_scale=scl[g][:, off : off + P],
+                        rhs=codes[g][:, off : off + P].bitcast(FP8X4),
+                        rhs_scale=scl[g][:, off : off + P],
+                        start=(a == 0),
+                        stop=(a == 1),
+                    )
+
+        def finish(g):
+            ost = outp.tile([P, GI * P], F32, name="ost%d" % g, tag="ost")
+            nc.scalar.activation(out=ost[:], in_=acc[g][:], func=ACT.Copy, scale=1.0 / K)
+            nc.sync.dma_start(
+                out=ov[:, GI * g : GI * g + GI, :], in_=ost[:].rearrange("p (i n) -> p i n", i=GI)
+            )
+
+        def live(g):
+            return 0 <= g < NG
+
+        for t in range(-2, NG + 2):
+            if live(t - 2):
+                finish(t - 2)
+            if live(t + 1):
+                mean(t + 1)
+            if live(t):
+                subtract(t)
+            if live(t + 2):
+                sum_scalar(t + 2, scalar_units(t + 2)[0])
+            if live(t):
+                transpose_and_copy(t)
+            if live(t - 1):
+                quantise(t - 1)
+                multiply(t - 1)
+            if live(t + 2):
+                for j in range(UNITS):
+                    if j not in scalar_units(t + 2):
+                        sum_vector(t + 2, j)
+                for j in scalar_units(t + 2)[1:]:
+                    sum_scalar(t + 2, j)

@@ -155,14 +155,15 @@ def tile_covpool_kernel(tc, x, out):
         def multiply(g):
             acc[g] = accp.tile([P, GI * P], F32, name="acc%d" % g, tag="acc")
             for i in range(GI):
+                width = 2 * P if i < GI - 1 else P
                 for a in range(2):
                     off = (a * GI + i) * P
                     nc.tensor.matmul_mx(
-                        out=acc[g][:, P * i : P * i + P],
+                        out=acc[g][:, P * i : P * i + width],
                         lhsT=codes[g][:, off : off + P].bitcast(FP8X4),
                         lhsT_scale=scl[g][:, off : off + P],
-                        rhs=codes[g][:, off : off + P].bitcast(FP8X4),
-                        rhs_scale=scl[g][:, off : off + P],
+                        rhs=codes[g][:, off : off + width].bitcast(FP8X4),
+                        rhs_scale=scl[g][:, off : off + width],
                         start=(a == 0),
                         stop=(a == 1),
                     )

@@ -130,40 +130,38 @@ def tile_covpool_kernel(tc, x, out):
                 )
 
         def transpose_and_copy(g):
-            grp[g] = grpp.tile([P, 2 * GI * HALF], BF16, name="grp%d" % g, tag="grp", align_bytes=64)
+            grp[g] = grpp.tile([P, 2, GI, HALF], BF16, name="grp%d" % g, tag="grp", align_bytes=64)
             for i in range(GI):
-                tp = tpp.tile([P, 4, P, 2], BF16, name="tp%d_%d" % (g, i), tag="tp")
+                tp = tpp.tile([P, 2, P, 2, 2], BF16, name="tp%d_%d" % (g, i), tag="tp")
                 for h in range(2):
-                    for v in range(4):
-                        nc.tensor.transpose(
-                            out=tp[:, v, 64 * h : 64 * h + 64, :].rearrange("p a u -> p (a u)"),
-                            in_=xc[g][:, 2 * i + h, P * v : P * v + P],
-                            identity=ident[:],
-                        )
-                for a in range(2):
-                    off = (a * GI + i) * HALF
-                    nc.scalar.copy(
-                        out=grp[g][:, off : off + HALF].rearrange("p (c v u) -> p c v u", v=2, u=2),
-                        in_=tp[:, 2 * a : 2 * a + 2, :, :].rearrange("p v c u -> p c v u"),
-                    )
+                    for a in range(2):
+                        for v in range(2):
+                            nc.tensor.transpose(
+                                out=tp[:, a, 64 * h : 64 * h + 64, v, :],
+                                in_=xc[g][:, 2 * i + h, P * (2 * a + v) : P * (2 * a + v) + P],
+                                identity=ident[:],
+                            )
+                nc.scalar.copy(
+                    out=grp[g][:, :, i, :],
+                    in_=tp[:].rearrange("p a c v u -> p a (c v u)"),
+                )
 
         def quantise(g):
             codes[g] = qp.tile([P, 2 * GI * P], U32, name="codes%d" % g, tag="codes", align_bytes=64)
             scl[g] = qp.tile([P, 2 * GI * P], U8, name="scl%d" % g, tag="scl", align_bytes=64)
-            nc.vector.quantize_mx(out=codes[g][:].bitcast(FP8X4), scales=scl[g][:], in_=grp[g][:])
+            nc.vector.quantize_mx(out=codes[g][:].bitcast(FP8X4), scales=scl[g][:], in_=grp[g][:].rearrange("p a i w -> p (a i w)"))
 
         def multiply(g):
             acc[g] = accp.tile([P, GI * P], F32, name="acc%d" % g, tag="acc")
             for i in range(GI):
-                width = 2 * P if i < GI - 1 else P
                 for a in range(2):
                     off = (a * GI + i) * P
                     nc.tensor.matmul_mx(
-                        out=acc[g][:, P * i : P * i + width],
+                        out=acc[g][:, P * i : P * i + P],
                         lhsT=codes[g][:, off : off + P].bitcast(FP8X4),
                         lhsT_scale=scl[g][:, off : off + P],
-                        rhs=codes[g][:, off : off + width].bitcast(FP8X4),
-                        rhs_scale=scl[g][:, off : off + width],
+                        rhs=codes[g][:, off : off + P].bitcast(FP8X4),
+                        rhs_scale=scl[g][:, off : off + P],
                         start=(a == 0),
                         stop=(a == 1),
                     )

@@ -24,7 +24,7 @@ SCOL = 8
 
 
 def scalar_units(g):
-    n = 3 if g % 2 == 0 else 2
+    n = 4
     return list(range(UNITS - n, UNITS))
 
 

@@ -24,7 +24,7 @@ SCOL = 8
 
 
 def scalar_units(g):
-    n = 4
+    n = 3 if g % 2 == 0 else 2
     return list(range(UNITS - n, UNITS))
 
 
@@ -85,13 +85,13 @@ def tile_covpool_kernel(tc, x, out):
             scalar2=None,
             op0=ALU.mult,
         )
-        junk_v = const.tile([P, HALF], BF16, name="junk_v")
-        junk_s = const.tile([P, HALF], BF16, name="junk_s")
+        junk_v = const.tile([P, UNITS, HALF], BF16, name="junk_v")
+        junk_s = const.tile([P, UNITS, HALF], BF16, name="junk_s")
 
         def sum_vector(g, j):
             c = column_of(g, j)
             nc.vector.tensor_scalar(
-                out=junk_v[:],
+                out=junk_v[:, j, :],
                 in0=xg[g][:, j, :],
                 scalar1=1.0,
                 scalar2=None,
@@ -103,7 +103,7 @@ def tile_covpool_kernel(tc, x, out):
         def sum_scalar(g, j):
             c = column_of(g, j)
             nc.scalar.activation(
-                out=junk_s[:], in_=xg[g][:, j, :], func=ACT.Copy, accum_out=sums[:, g, c : c + 1]
+                out=junk_s[:, j, :], in_=xg[g][:, j, :], func=ACT.Copy, accum_out=sums[:, g, c : c + 1]
             )
 
         def mean(g):

@@ -24,7 +24,7 @@ SCOL = 8
 
 
 def scalar_units(g):
-    n = 3 if g % 2 == 0 else 2
+    n = 1
     return list(range(UNITS - n, UNITS))
 
 

@@ -16,40 +16,33 @@ ACT = mybir.ActivationFunctionType
 P = 128
 B = 64
 K = 1024
-HALF = 512
+UI = 2
+NU = B // UI
 GI = 4
 NG = B // GI
-UNITS = 2 * GI
-SCOL = 8
+AHEAD = 8
 
 
-def scalar_units(g):
-    n = 1
-    return list(range(UNITS - n, UNITS))
-
-
-def column_of(g, j):
-    su = scalar_units(g)
-    if j in su:
-        return SCOL + su.index(j)
-    return j
+def on_scalar(b):
+    return b % 3 == 2
 
 
 def tile_covpool_kernel(tc, x, out):
     nc = tc.nc
-    xv = x.rearrange("b c y z -> (b c y z)").rearrange("(s q j) -> q s j", s=2 * B, q=P, j=HALF)
+    xv = x.rearrange("b c y z -> c b (y z)")
     ov = out.rearrange("b c n -> c b n")
 
     with ExitStack() as ctx:
         const = ctx.enter_context(tc.tile_pool(name="const", bufs=1))
         xin = ctx.enter_context(tc.tile_pool(name="xin", bufs=1))
+        junkv = ctx.enter_context(tc.tile_pool(name="junkv", bufs=4))
+        junks = ctx.enter_context(tc.tile_pool(name="junks", bufs=4))
         xcp = ctx.enter_context(tc.tile_pool(name="xcp", bufs=3))
         grpp = ctx.enter_context(tc.tile_pool(name="grpp", bufs=3))
-        qp = ctx.enter_context(tc.tile_pool(name="qp", bufs=2))
+        qp = ctx.enter_context(tc.tile_pool(name="qp", bufs=3))
         outp = ctx.enter_context(tc.tile_pool(name="outp", bufs=4))
         tpp = ctx.enter_context(tc.psum_pool(name="tpp", bufs=5))
-        accp = ctx.enter_context(tc.psum_pool(name="accp", bufs=2))
-        msp = ctx.enter_context(tc.psum_pool(name="msp", bufs=1))
+        accp = ctx.enter_context(tc.psum_pool(name="accp", bufs=3))
         ctx.enter_context(tc.manual_schedule())
 
         xg = {}
@@ -59,140 +52,118 @@ def tile_covpool_kernel(tc, x, out):
         scl = {}
         acc = {}
 
-        for g in range(NG):
-            xg[g] = xin.tile([P, UNITS, HALF], BF16, name="x%d" % g, tag="x%d" % g)
-            pieces = 4 if g == 0 else (2 if g == 1 else 1)
-            step = UNITS // pieces
-            for a in range(0, UNITS, step):
-                nc.sync.dma_start(
-                    out=xg[g][:, a : a + step, :],
-                    in_=xv[:, UNITS * g + a : UNITS * g + a + step, :],
+        def load(g):
+            xg[g] = xin.tile([P, GI, K], BF16, name="x%d" % g, tag="x%d" % g)
+            step = 1 if g == 0 else (2 if g == 1 else 4)
+            for a in range(0, GI, step):
+                nc.sync.dma_start(out=xg[g][:, a : a + step, :], in_=xv[:, GI * g + a : GI * g + a + step, :])
+
+        for g in range(AHEAD):
+            load(g)
+
+        ident = const.tile([P, P], F32, name="ident")
+        make_identity(nc, ident[:])
+        negmean = {}
+
+        def image(b):
+            return xg[b // GI][:, b % GI, :]
+
+        def sum_of(b):
+            negmean[b] = const.tile([P, 1], F32, name="nm%d" % b, tag="nm%d" % b)
+            if on_scalar(b):
+                js = junks.tile([P, K], BF16, name="js%d" % b, tag="js")
+                nc.scalar.activation(
+                    out=js[:], in_=image(b), func=ACT.Copy, scale=-1.0 / K, accum_out=negmean[b][:]
+                )
+            else:
+                jv = junkv.tile([P, K], BF16, name="jv%d" % b, tag="jv")
+                nc.vector.tensor_scalar(
+                    out=jv[:],
+                    in0=image(b),
+                    scalar1=-1.0 / K,
+                    scalar2=None,
+                    op0=ALU.mult,
+                    op1=ALU.add,
+                    accum_out=negmean[b][:],
                 )
 
-        ident = const.tile([P, P], BF16, name="ident")
-        make_identity(nc, ident[:])
-        sums = const.tile([P, NG, 16], F32, name="sums")
-        nc.vector.memset(sums[:], 0.0)
-        negmean = const.tile([P, NG, 16], F32, name="negmean")
-        idv = ident[:].rearrange("p (a e) -> p a e", e=2)
-        pairs = const.tile([P, P // 2, 1], F32, name="pairs")
-        nc.vector.tensor_tensor(out=pairs[:], in0=idv[:, :, 0:1], in1=idv[:, :, 1:2], op=ALU.add)
-        gp = const.tile([P, P // 2, 2], F32, name="gp")
-        nc.vector.tensor_scalar(
-            out=gp[:],
-            in0=pairs[:].to_broadcast([P, P // 2, 2]),
-            scalar1=-1.0 / K,
-            scalar2=None,
-            op0=ALU.mult,
-        )
-        junk_v = const.tile([P, UNITS, HALF], BF16, name="junk_v")
-        junk_s = const.tile([P, UNITS, HALF], BF16, name="junk_s")
-
-        def sum_vector(g, j):
-            c = column_of(g, j)
-            nc.vector.tensor_scalar(
-                out=junk_v[:, j, :],
-                in0=xg[g][:, j, :],
-                scalar1=1.0,
-                scalar2=None,
-                op0=ALU.mult,
-                op1=ALU.add,
-                accum_out=sums[:, g, c : c + 1],
-            )
-
-        def sum_scalar(g, j):
-            c = column_of(g, j)
-            nc.scalar.activation(
-                out=junk_s[:, j, :], in_=xg[g][:, j, :], func=ACT.Copy, accum_out=sums[:, g, c : c + 1]
-            )
-
-        def mean(g):
-            ms = msp.tile([P, 16], F32, name="ms%d" % g, tag="ms")
-            nc.tensor.matmul(
-                out=ms[:],
-                lhsT=gp[:].rearrange("p a e -> p (a e)"),
-                rhs=sums[:, g, :],
-                start=True,
-                stop=True,
-            )
-            nc.scalar.copy(out=negmean[:, g, :], in_=ms[:])
-
-        def subtract(g):
-            xc[g] = xcp.tile([P, UNITS, HALF], BF16, name="xc%d" % g, tag="xc")
-            for j in range(UNITS):
-                c = column_of(g, j)
+        def subtract(u):
+            xc[u] = xcp.tile([P, UI, K], BF16, name="xc%d" % u, tag="xc")
+            for i in range(UI):
+                b = UI * u + i
                 nc.vector.tensor_scalar(
-                    out=xc[g][:, j, :],
-                    in0=xg[g][:, j, :],
-                    scalar1=negmean[:, g, c : c + 1],
+                    out=xc[u][:, i, :],
+                    in0=image(b),
+                    scalar1=negmean[b][:],
                     scalar2=None,
                     op0=ALU.add,
                 )
 
-        def transpose_and_copy(g):
-            grp[g] = grpp.tile([P, 2, GI, HALF], BF16, name="grp%d" % g, tag="grp", align_bytes=64)
-            for i in range(GI):
-                tp = tpp.tile([P, 2, P, 2, 2], BF16, name="tp%d_%d" % (g, i), tag="tp")
-                for h in range(2):
-                    for a in range(2):
-                        for v in range(2):
-                            nc.tensor.transpose(
-                                out=tp[:, a, 64 * h : 64 * h + 64, v, :],
-                                in_=xc[g][:, 2 * i + h, P * (2 * a + v) : P * (2 * a + v) + P],
-                                identity=ident[:],
-                            )
+        def transpose(u):
+            tp = []
+            for i in range(UI):
+                words = xc[u][:, i, :].bitcast(F32)
+                t = tpp.tile([P, 4, P], F32, name="tp%d_%d" % (u, i), tag="tp")
+                for q in range(4):
+                    nc.tensor.transpose(out=t[:, q, :], in_=words[:, P * q : P * q + P], identity=ident[:])
+                tp.append(t)
+            return tp
+
+        def copy_out(u, tp):
+            grp[u] = grpp.tile([P, UI, K], BF16, name="grp%d" % u, tag="grp", align_bytes=64)
+            for i in range(UI):
                 nc.scalar.copy(
-                    out=grp[g][:, :, i, :],
-                    in_=tp[:].rearrange("p a c v u -> p a (c v u)"),
+                    out=grp[u][:, i, :].bitcast(F32).rearrange("p (a c u) -> p a c u", a=2, u=2),
+                    in_=tp[i][:].rearrange("p (a u) c -> p a c u", a=2),
                 )
 
-        def quantise(g):
-            codes[g] = qp.tile([P, 2 * GI * P], U32, name="codes%d" % g, tag="codes", align_bytes=64)
-            scl[g] = qp.tile([P, 2 * GI * P], U8, name="scl%d" % g, tag="scl", align_bytes=64)
-            nc.vector.quantize_mx(out=codes[g][:].bitcast(FP8X4), scales=scl[g][:], in_=grp[g][:].rearrange("p a i w -> p (a i w)"))
+        def quantise(u):
+            codes[u] = qp.tile([P, UI * 2 * P], U32, name="codes%d" % u, tag="codes", align_bytes=64)
+            scl[u] = qp.tile([P, UI * 2 * P], U8, name="scl%d" % u, tag="scl", align_bytes=64)
+            nc.vector.quantize_mx(
+                out=codes[u][:].bitcast(FP8X4), scales=scl[u][:], in_=grp[u][:].rearrange("p i w -> p (i w)")
+            )
 
-        def multiply(g):
-            acc[g] = accp.tile([P, GI * P], F32, name="acc%d" % g, tag="acc")
-            for i in range(GI):
+        def multiply(u):
+            g = UI * u // GI
+            if UI * u % GI == 0:
+                acc[g] = accp.tile([P, GI, P], F32, name="acc%d" % g, tag="acc")
+            for i in range(UI):
                 for a in range(2):
-                    off = (a * GI + i) * P
+                    off = (2 * i + a) * P
                     nc.tensor.matmul_mx(
-                        out=acc[g][:, P * i : P * i + P],
-                        lhsT=codes[g][:, off : off + P].bitcast(FP8X4),
-                        lhsT_scale=scl[g][:, off : off + P],
-                        rhs=codes[g][:, off : off + P].bitcast(FP8X4),
-                        rhs_scale=scl[g][:, off : off + P],
+                        out=acc[g][:, (UI * u + i) % GI, :],
+                        lhsT=codes[u][:, off : off + P].bitcast(FP8X4),
+                        lhsT_scale=scl[u][:, off : off + P],
+                        rhs=codes[u][:, off : off + P].bitcast(FP8X4),
+                        rhs_scale=scl[u][:, off : off + P],
                         start=(a == 0),
                         stop=(a == 1),
                     )
 
         def finish(g):
-            ost = outp.tile([P, GI * P], F32, name="ost%d" % g, tag="ost")
+            ost = outp.tile([P, GI, P], F32, name="ost%d" % g, tag="ost")
             nc.scalar.activation(out=ost[:], in_=acc[g][:], func=ACT.Copy, scale=1.0 / K)
-            nc.sync.dma_start(
-                out=ov[:, GI * g : GI * g + GI, :], in_=ost[:].rearrange("p (i n) -> p i n", i=GI)
-            )
+            nc.sync.dma_start(out=ov[:, GI * g : GI * g + GI, :], in_=ost[:])
 
-        def live(g):
-            return 0 <= g < NG
+        def live(u):
+            return 0 <= u < NU
 
-        for t in range(-2, NG + 2):
-            if live(t - 2):
-                finish(t - 2)
-            if live(t + 1):
-                mean(t + 1)
-            if live(t):
-                subtract(t)
-            if live(t + 2):
-                sum_scalar(t + 2, scalar_units(t + 2)[0])
-            if live(t):
-                transpose_and_copy(t)
+        for t in range(-2, NU + 3):
             if live(t - 1):
                 quantise(t - 1)
-                multiply(t - 1)
+            if live(t + 1):
+                subtract(t + 1)
+            if live(t):
+                tp = transpose(t)
+                copy_out(t, tp)
             if live(t + 2):
-                for j in range(UNITS):
-                    if j not in scalar_units(t + 2):
-                        sum_vector(t + 2, j)
-                for j in scalar_units(t + 2)[1:]:
-                    sum_scalar(t + 2, j)
+                for i in range(UI):
+                    sum_of(UI * (t + 2) + i)
+            if live(t - 1):
+                multiply(t - 1)
+            if live(t - 2) and (t - 2) % 2 == 1:
+                g = (t - 2) // 2
+                finish(g)
+                if g + AHEAD < NG:
+                    load(g + AHEAD)

@@ -24,7 +24,7 @@ AHEAD = 8
 
 
 def on_scalar(b):
-    return b % 3 == 2
+    return b % 4 == 3
 
 
 def tile_covpool_kernel(tc, x, out):

@@ -21,6 +21,7 @@ NU = B // UI
 GI = 4
 NG = B // GI
 AHEAD = 8
+WARM = 160
 
 
 def on_scalar(b):
@@ -42,7 +43,8 @@ def tile_covpool_kernel(tc, x, out):
         qp = ctx.enter_context(tc.tile_pool(name="qp", bufs=3))
         outp = ctx.enter_context(tc.tile_pool(name="outp", bufs=4))
         tpp = ctx.enter_context(tc.psum_pool(name="tpp", bufs=5))
-        accp = ctx.enter_context(tc.psum_pool(name="accp", bufs=3))
+        accp = ctx.enter_context(tc.psum_pool(name="accp", bufs=2))
+        warmp = ctx.enter_context(tc.psum_pool(name="warmp", bufs=1))
         ctx.enter_context(tc.manual_schedule())
 
         xg = {}
@@ -64,6 +66,9 @@ def tile_covpool_kernel(tc, x, out):
         ident = const.tile([P, P], F32, name="ident")
         make_identity(nc, ident[:])
         negmean = {}
+        filler = const.tile([P, WARM], F32, name="filler")
+        nc.gpsimd.memset(filler[:], 0.0)
+        warm = warmp.tile([P, WARM], F32, name="warm")
 
         def image(b):
             return xg[b // GI][:, b % GI, :]
@@ -157,6 +162,8 @@ def tile_covpool_kernel(tc, x, out):
             if live(t):
                 tp = transpose(t)
                 copy_out(t, tp)
+            if live(t):
+                nc.tensor.matmul(out=warm[:], lhsT=ident[:], rhs=filler[:], start=True, stop=True)
             if live(t + 2):
                 for i in range(UI):
                     sum_of(UI * (t + 2) + i)

@@ -39,7 +39,7 @@ def tile_covpool_kernel(tc, x, out):
         junkv = ctx.enter_context(tc.tile_pool(name="junkv", bufs=4))
         junks = ctx.enter_context(tc.tile_pool(name="junks", bufs=4))
         xcp = ctx.enter_context(tc.tile_pool(name="xcp", bufs=3))
-        grpp = ctx.enter_context(tc.tile_pool(name="grpp", bufs=3))
+        grpp = ctx.enter_context(tc.tile_pool(name="grpp", bufs=4))
         qp = ctx.enter_context(tc.tile_pool(name="qp", bufs=3))
         outp = ctx.enter_context(tc.tile_pool(name="outp", bufs=4))
         tpp = ctx.enter_context(tc.psum_pool(name="tpp", bufs=5))
@@ -154,9 +154,9 @@ def tile_covpool_kernel(tc, x, out):
         def live(u):
             return 0 <= u < NU
 
-        for t in range(-2, NU + 3):
-            if live(t - 1):
-                quantise(t - 1)
+        for t in range(-2, NU + 4):
+            if live(t - 2):
+                quantise(t - 2)
             if live(t + 1):
                 subtract(t + 1)
             if live(t):
@@ -167,10 +167,10 @@ def tile_covpool_kernel(tc, x, out):
             if live(t + 2):
                 for i in range(UI):
                     sum_of(UI * (t + 2) + i)
-            if live(t - 1):
-                multiply(t - 1)
-            if live(t - 2) and (t - 2) % 2 == 1:
-                g = (t - 2) // 2
+            if live(t - 2):
+                multiply(t - 2)
+            if live(t - 3) and (t - 3) % 2 == 1:
+                g = (t - 3) // 2
                 finish(g)
                 if g + AHEAD < NG:
                     load(g + AHEAD)

@@ -21,11 +21,18 @@ NU = B // UI
 GI = 4
 NG = B // GI
 AHEAD = 8
-WARM = 160
 
 
 def on_scalar(b):
     return b % 4 == 3
+
+
+def on_gpsimd(b):
+    return b % 4 == 3
+
+
+def is_folded(b):
+    return b % 12 == 3
 
 
 def tile_covpool_kernel(tc, x, out):
@@ -44,7 +51,7 @@ def tile_covpool_kernel(tc, x, out):
         outp = ctx.enter_context(tc.tile_pool(name="outp", bufs=4))
         tpp = ctx.enter_context(tc.psum_pool(name="tpp", bufs=5))
         accp = ctx.enter_context(tc.psum_pool(name="accp", bufs=2))
-        warmp = ctx.enter_context(tc.psum_pool(name="warmp", bufs=1))
+        foldp = ctx.enter_context(tc.psum_pool(name="foldp", bufs=1))
         ctx.enter_context(tc.manual_schedule())
 
         xg = {}
@@ -66,16 +73,21 @@ def tile_covpool_kernel(tc, x, out):
         ident = const.tile([P, P], F32, name="ident")
         make_identity(nc, ident[:])
         negmean = {}
-        filler = const.tile([P, WARM], F32, name="filler")
-        nc.gpsimd.memset(filler[:], 0.0)
-        warm = warmp.tile([P, WARM], F32, name="warm")
+        ident16 = const.tile([P, P], BF16, name="ident16")
+        nc.gpsimd.tensor_copy(out=ident16[:], in_=ident[:])
+        folded = {}
 
         def image(b):
             return xg[b // GI][:, b % GI, :]
 
         def sum_of(b):
             negmean[b] = const.tile([P, 1], F32, name="nm%d" % b, tag="nm%d" % b)
-            if on_scalar(b):
+            if is_folded(b):
+                js = junks.tile([P, P], BF16, name="jf%d" % b, tag="jf")
+                nc.scalar.activation(
+                    out=js[:], in_=folded[b][:], func=ACT.Copy, scale=-1.0 / K, accum_out=negmean[b][:]
+                )
+            elif on_scalar(b):
                 js = junks.tile([P, K], BF16, name="js%d" % b, tag="js")
                 nc.scalar.activation(
                     out=js[:], in_=image(b), func=ACT.Copy, scale=-1.0 / K, accum_out=negmean[b][:]
@@ -92,17 +104,40 @@ def tile_covpool_kernel(tc, x, out):
                     accum_out=negmean[b][:],
                 )
 
+        def fold(b):
+            folded[b] = foldp.tile([P, P], F32, name="fold%d" % b, tag="fold")
+            for q in range(K // P):
+                nc.tensor.matmul(
+                    out=folded[b][:],
+                    lhsT=ident16[:],
+                    rhs=image(b)[:, P * q : P * q + P],
+                    start=(q == 0),
+                    stop=(q == K // P - 1),
+                )
+
         def subtract(u):
             xc[u] = xcp.tile([P, UI, K], BF16, name="xc%d" % u, tag="xc")
             for i in range(UI):
                 b = UI * u + i
-                nc.vector.tensor_scalar(
-                    out=xc[u][:, i, :],
-                    in0=image(b),
-                    scalar1=negmean[b][:],
-                    scalar2=None,
-                    op0=ALU.add,
-                )
+                if on_gpsimd(b):
+                    nc.gpsimd.tensor_scalar(
+                        out=xc[u][:, i, :],
+                        in0=image(b),
+                        scalar1=negmean[b][:],
+                        scalar2=1.0,
+                        op0=ALU.add,
+                        op1=ALU.mult,
+                    )
+                else:
+                    spill = 2 if on_gpsimd(b + 1) else 0
+                    start = b % GI * K
+                    nc.vector.tensor_scalar(
+                        out=xc[u][:].rearrange("p i k -> p (i k)")[:, i * K : i * K + K + spill],
+                        in0=xg[b // GI][:].rearrange("p i k -> p (i k)")[:, start : start + K + spill],
+                        scalar1=negmean[b][:],
+                        scalar2=None,
+                        op0=ALU.add,
+                    )
 
         def transpose(u):
             tp = []
@@ -114,13 +149,13 @@ def tile_covpool_kernel(tc, x, out):
                 tp.append(t)
             return tp
 
-        def copy_out(u, tp):
-            grp[u] = grpp.tile([P, UI, K], BF16, name="grp%d" % u, tag="grp", align_bytes=64)
-            for i in range(UI):
-                nc.scalar.copy(
-                    out=grp[u][:, i, :].bitcast(F32).rearrange("p (a c u) -> p a c u", a=2, u=2),
-                    in_=tp[i][:].rearrange("p (a u) c -> p a c u", a=2),
-                )
+        def copy_out(u, tp, i):
+            if i == 0:
+                grp[u] = grpp.tile([P, UI, K], BF16, name="grp%d" % u, tag="grp", align_bytes=64)
+            nc.scalar.copy(
+                out=grp[u][:, i, :].bitcast(F32).rearrange("p (a c u) -> p a c u", a=2, u=2),
+                in_=tp[i][:].rearrange("p (a u) c -> p a c u", a=2),
+            )
 
         def quantise(u):
             codes[u] = qp.tile([P, UI * 2 * P], U32, name="codes%d" % u, tag="codes", align_bytes=64)
@@ -161,12 +196,16 @@ def tile_covpool_kernel(tc, x, out):
                 subtract(t + 1)
             if live(t):
                 tp = transpose(t)
-                copy_out(t, tp)
-            if live(t):
-                nc.tensor.matmul(out=warm[:], lhsT=ident[:], rhs=filler[:], start=True, stop=True)
+                copy_out(t, tp, 0)
+            if live(t + 2):
+                for i in range(UI):
+                    if is_folded(UI * (t + 2) + i):
+                        fold(UI * (t + 2) + i)
             if live(t + 2):
                 for i in range(UI):
                     sum_of(UI * (t + 2) + i)
+            if live(t):
+                copy_out(t, tp, 1)
             if live(t - 2):
                 multiply(t - 2)
             if live(t - 3) and (t - 3) % 2 == 1:

@@ -27,12 +27,8 @@ def on_scalar(b):
     return b % 4 == 3
 
 
-def on_gpsimd(b):
-    return b % 4 == 3
-
-
 def is_folded(b):
-    return b % 12 == 3
+    return b % 10 == 6
 
 
 def tile_covpool_kernel(tc, x, out):
@@ -119,25 +115,13 @@ def tile_covpool_kernel(tc, x, out):
             xc[u] = xcp.tile([P, UI, K], BF16, name="xc%d" % u, tag="xc")
             for i in range(UI):
                 b = UI * u + i
-                if on_gpsimd(b):
-                    nc.gpsimd.tensor_scalar(
-                        out=xc[u][:, i, :],
-                        in0=image(b),
-                        scalar1=negmean[b][:],
-                        scalar2=1.0,
-                        op0=ALU.add,
-                        op1=ALU.mult,
-                    )
-                else:
-                    spill = 2 if on_gpsimd(b + 1) else 0
-                    start = b % GI * K
-                    nc.vector.tensor_scalar(
-                        out=xc[u][:].rearrange("p i k -> p (i k)")[:, i * K : i * K + K + spill],
-                        in0=xg[b // GI][:].rearrange("p i k -> p (i k)")[:, start : start + K + spill],
-                        scalar1=negmean[b][:],
-                        scalar2=None,
-                        op0=ALU.add,
-                    )
+                nc.vector.tensor_scalar(
+                    out=xc[u][:, i, :],
+                    in0=image(b),
+                    scalar1=negmean[b][:],
+                    scalar2=None,
+                    op0=ALU.add,
+                )
 
         def transpose(u):
             tp = []

@@ -28,7 +28,16 @@ def on_scalar(b):
 
 
 def is_folded(b):
-    return b % 10 == 6
+    return b % 10 == 2 and b > 2
+
+
+def sum_step(b):
+    u = b // UI
+    if is_folded(b):
+        return u - 3
+    if on_scalar(b):
+        return max(u - 4, (u - 3) // 2)
+    return u - 2
 
 
 def tile_covpool_kernel(tc, x, out):
@@ -181,13 +190,12 @@ def tile_covpool_kernel(tc, x, out):
             if live(t):
                 tp = transpose(t)
                 copy_out(t, tp, 0)
-            if live(t + 2):
-                for i in range(UI):
-                    if is_folded(UI * (t + 2) + i):
-                        fold(UI * (t + 2) + i)
-            if live(t + 2):
-                for i in range(UI):
-                    sum_of(UI * (t + 2) + i)
+            for b in range(B):
+                if is_folded(b) and b // UI - 4 == t:
+                    fold(b)
+            for b in range(B):
+                if sum_step(b) == t:
+                    sum_of(b)
             if live(t):
                 copy_out(t, tp, 1)
             if live(t - 2):

@@ -20,6 +20,7 @@ UI = 2
 NU = B // UI
 GI = 4
 NG = B // GI
+WORDS = 2 * P
 AHEAD = 8
 
 
@@ -28,16 +29,20 @@ def on_scalar(b):
 
 
 def is_folded(b):
-    return b % 10 == 2 and b > 2
+    return b % 10 == 0 and b > 0
 
 
 def sum_step(b):
     u = b // UI
-    if is_folded(b):
-        return u - 3
-    if on_scalar(b):
-        return max(u - 4, (u - 3) // 2)
-    return u - 2
+    return u - 3 if on_scalar(b) and u >= 2 else u - 2
+
+
+def fold_step(b):
+    return b // UI - 3
+
+
+def pieces(g):
+    return [(0, 2), (2, 3), (3, 4)] if g == NG - 1 else [(0, GI)]
 
 
 def tile_covpool_kernel(tc, x, out):
@@ -48,11 +53,11 @@ def tile_covpool_kernel(tc, x, out):
     with ExitStack() as ctx:
         const = ctx.enter_context(tc.tile_pool(name="const", bufs=1))
         xin = ctx.enter_context(tc.tile_pool(name="xin", bufs=1))
-        junkv = ctx.enter_context(tc.tile_pool(name="junkv", bufs=4))
+        junkv = ctx.enter_context(tc.tile_pool(name="junkv", bufs=8))
         junks = ctx.enter_context(tc.tile_pool(name="junks", bufs=4))
         xcp = ctx.enter_context(tc.tile_pool(name="xcp", bufs=3))
         grpp = ctx.enter_context(tc.tile_pool(name="grpp", bufs=4))
-        qp = ctx.enter_context(tc.tile_pool(name="qp", bufs=3))
+        qp = ctx.enter_context(tc.tile_pool(name="qp", bufs=2))
         outp = ctx.enter_context(tc.tile_pool(name="outp", bufs=4))
         tpp = ctx.enter_context(tc.psum_pool(name="tpp", bufs=5))
         accp = ctx.enter_context(tc.psum_pool(name="accp", bufs=2))
@@ -61,41 +66,51 @@ def tile_covpool_kernel(tc, x, out):
 
         xg = {}
         xc = {}
+        tp = {}
         grp = {}
         codes = {}
         scl = {}
         acc = {}
+        ost = {}
+        negmean = {}
+        folded = {}
 
         def load(g):
             xg[g] = xin.tile([P, GI, K], BF16, name="x%d" % g, tag="x%d" % g)
-            step = 1 if g == 0 else (2 if g == 1 else 4)
-            for a in range(0, GI, step):
-                nc.sync.dma_start(out=xg[g][:, a : a + step, :], in_=xv[:, GI * g + a : GI * g + a + step, :])
+            cuts = {0: [0, 1, 2, 4], 1: [0, 2, 4]}.get(g, [0, 4])
+            for lo, hi in zip(cuts[:-1], cuts[1:]):
+                nc.sync.dma_start(out=xg[g][:, lo:hi, :], in_=xv[:, GI * g + lo : GI * g + hi, :])
 
         for g in range(AHEAD):
             load(g)
 
         ident = const.tile([P, P], F32, name="ident")
         make_identity(nc, ident[:])
-        negmean = {}
         ident16 = const.tile([P, P], BF16, name="ident16")
         nc.gpsimd.tensor_copy(out=ident16[:], in_=ident[:])
-        folded = {}
 
         def image(b):
             return xg[b // GI][:, b % GI, :]
 
+        def fold(b):
+            folded[b] = foldp.tile([P, P], F32, name="fold%d" % b, tag="fold")
+            for q in range(K // P):
+                nc.tensor.matmul(
+                    out=folded[b][:],
+                    lhsT=ident16[:],
+                    rhs=image(b)[:, P * q : P * q + P],
+                    start=(q == 0),
+                    stop=(q == K // P - 1),
+                )
+
         def sum_of(b):
             negmean[b] = const.tile([P, 1], F32, name="nm%d" % b, tag="nm%d" % b)
-            if is_folded(b):
-                js = junks.tile([P, P], BF16, name="jf%d" % b, tag="jf")
-                nc.scalar.activation(
-                    out=js[:], in_=folded[b][:], func=ACT.Copy, scale=-1.0 / K, accum_out=negmean[b][:]
-                )
-            elif on_scalar(b):
+            if is_folded(b) or on_scalar(b):
+                source = folded[b][:] if is_folded(b) else image(b)
+                n = P if is_folded(b) else K
                 js = junks.tile([P, K], BF16, name="js%d" % b, tag="js")
                 nc.scalar.activation(
-                    out=js[:], in_=image(b), func=ACT.Copy, scale=-1.0 / K, accum_out=negmean[b][:]
+                    out=js[:, 0:n], in_=source, func=ACT.Copy, scale=-1.0 / K, accum_out=negmean[b][:]
                 )
             else:
                 jv = junkv.tile([P, K], BF16, name="jv%d" % b, tag="jv")
@@ -107,17 +122,6 @@ def tile_covpool_kernel(tc, x, out):
                     op0=ALU.mult,
                     op1=ALU.add,
                     accum_out=negmean[b][:],
-                )
-
-        def fold(b):
-            folded[b] = foldp.tile([P, P], F32, name="fold%d" % b, tag="fold")
-            for q in range(K // P):
-                nc.tensor.matmul(
-                    out=folded[b][:],
-                    lhsT=ident16[:],
-                    rhs=image(b)[:, P * q : P * q + P],
-                    start=(q == 0),
-                    stop=(q == K // P - 1),
                 )
 
         def subtract(u):
@@ -133,75 +137,87 @@ def tile_covpool_kernel(tc, x, out):
                 )
 
         def transpose(u):
-            tp = []
             for i in range(UI):
                 words = xc[u][:, i, :].bitcast(F32)
                 t = tpp.tile([P, 4, P], F32, name="tp%d_%d" % (u, i), tag="tp")
                 for q in range(4):
                     nc.tensor.transpose(out=t[:, q, :], in_=words[:, P * q : P * q + P], identity=ident[:])
-                tp.append(t)
-            return tp
+                tp[UI * u + i] = t
 
-        def copy_out(u, tp, i):
-            if i == 0:
-                grp[u] = grpp.tile([P, UI, K], BF16, name="grp%d" % u, tag="grp", align_bytes=64)
-            nc.scalar.copy(
-                out=grp[u][:, i, :].bitcast(F32).rearrange("p (a c u) -> p a c u", a=2, u=2),
-                in_=tp[i][:].rearrange("p (a u) c -> p a c u", a=2),
-            )
-
-        def quantise(u):
-            codes[u] = qp.tile([P, UI * 2 * P], U32, name="codes%d" % u, tag="codes", align_bytes=64)
-            scl[u] = qp.tile([P, UI * 2 * P], U8, name="scl%d" % u, tag="scl", align_bytes=64)
-            nc.vector.quantize_mx(
-                out=codes[u][:].bitcast(FP8X4), scales=scl[u][:], in_=grp[u][:].rearrange("p i w -> p (i w)")
-            )
-
-        def multiply(u):
+        def copy_out(u):
             g = UI * u // GI
             if UI * u % GI == 0:
+                grp[g] = grpp.tile([P, GI, K], BF16, name="grp%d" % g, tag="grp", align_bytes=64)
+            for i in reversed(range(UI)):
+                b = UI * u + i
+                nc.scalar.copy(
+                    out=grp[g][:, b % GI, :].bitcast(F32).rearrange("p (a c u) -> p a c u", a=2, u=2),
+                    in_=tp[b][:].rearrange("p (a u) c -> p a c u", a=2),
+                )
+
+        def quantise(g, lo, hi):
+            if lo == 0:
+                codes[g] = qp.tile([P, GI * WORDS], U32, name="codes%d" % g, tag="codes", align_bytes=64)
+                scl[g] = qp.tile([P, GI * WORDS], U8, name="scl%d" % g, tag="scl", align_bytes=64)
+            nc.vector.quantize_mx(
+                out=codes[g][:, WORDS * lo : WORDS * hi].bitcast(FP8X4),
+                scales=scl[g][:, WORDS * lo : WORDS * hi],
+                in_=grp[g][:, lo:hi, :].rearrange("p i w -> p (i w)"),
+            )
+
+        def multiply(g, lo, hi):
+            if lo == 0:
                 acc[g] = accp.tile([P, GI, P], F32, name="acc%d" % g, tag="acc")
-            for i in range(UI):
+            for i in range(lo, hi):
                 for a in range(2):
-                    off = (2 * i + a) * P
+                    off = WORDS * i + P * a
                     nc.tensor.matmul_mx(
-                        out=acc[g][:, (UI * u + i) % GI, :],
-                        lhsT=codes[u][:, off : off + P].bitcast(FP8X4),
-                        lhsT_scale=scl[u][:, off : off + P],
-                        rhs=codes[u][:, off : off + P].bitcast(FP8X4),
-                        rhs_scale=scl[u][:, off : off + P],
+                        out=acc[g][:, i, :],
+                        lhsT=codes[g][:, off : off + P].bitcast(FP8X4),
+                        lhsT_scale=scl[g][:, off : off + P],
+                        rhs=codes[g][:, off : off + P].bitcast(FP8X4),
+                        rhs_scale=scl[g][:, off : off + P],
                         start=(a == 0),
                         stop=(a == 1),
                     )
 
-        def finish(g):
-            ost = outp.tile([P, GI, P], F32, name="ost%d" % g, tag="ost")
-            nc.scalar.activation(out=ost[:], in_=acc[g][:], func=ACT.Copy, scale=1.0 / K)
-            nc.sync.dma_start(out=ov[:, GI * g : GI * g + GI, :], in_=ost[:])
+        def finish(g, lo, hi):
+            if lo == 0:
+                ost[g] = outp.tile([P, GI, P], F32, name="ost%d" % g, tag="ost")
+            nc.scalar.activation(out=ost[g][:, lo:hi, :], in_=acc[g][:, lo:hi, :], func=ACT.Copy, scale=1.0 / K)
+            nc.sync.dma_start(out=ov[:, GI * g + lo : GI * g + hi, :], in_=ost[g][:, lo:hi, :])
 
         def live(u):
             return 0 <= u < NU
 
-        for t in range(-2, NU + 4):
-            if live(t - 2):
-                quantise(t - 2)
+        def group_at(t, lag):
+            g, odd = divmod(t - lag, 2)
+            return g if odd == 0 and 0 <= g < NG else None
+
+        for t in range(-2, NU + 7):
             if live(t + 1):
                 subtract(t + 1)
+            g = group_at(t, 3)
+            if g is not None:
+                for lo, hi in pieces(g):
+                    quantise(g, lo, hi)
             if live(t):
-                tp = transpose(t)
-                copy_out(t, tp, 0)
+                transpose(t)
+            if live(t):
+                copy_out(t)
             for b in range(B):
-                if is_folded(b) and b // UI - 4 == t:
+                if is_folded(b) and fold_step(b) == t:
                     fold(b)
             for b in range(B):
                 if sum_step(b) == t:
                     sum_of(b)
-            if live(t):
-                copy_out(t, tp, 1)
-            if live(t - 2):
-                multiply(t - 2)
-            if live(t - 3) and (t - 3) % 2 == 1:
-                g = (t - 3) // 2
-                finish(g)
+            g = group_at(t, 4)
+            if g is not None:
+                for lo, hi in pieces(g):
+                    multiply(g, lo, hi)
+            g = group_at(t, 5)
+            if g is not None:
+                for lo, hi in pieces(g):
+                    finish(g, lo, hi)
                 if g + AHEAD < NG:
                     load(g + AHEAD)

@@ -16,8 +16,6 @@ ACT = mybir.ActivationFunctionType
 P = 128
 B = 64
 K = 1024
-UI = 2
-NU = B // UI
 GI = 4
 NG = B // GI
 WORDS = 2 * P
@@ -29,16 +27,15 @@ def on_scalar(b):
 
 
 def is_folded(b):
-    return b % 10 == 0 and b > 0
+    return b % 12 == 11
 
 
-def sum_step(b):
-    u = b // UI
-    return u - 3 if on_scalar(b) and u >= 2 else u - 2
+def on_gpsimd(b):
+    return b % 4 == 3 and 0 < b // GI < NG - 1
 
 
-def fold_step(b):
-    return b // UI - 3
+def copied_by_vector(b):
+    return b == B - 1
 
 
 def pieces(g):
@@ -53,15 +50,14 @@ def tile_covpool_kernel(tc, x, out):
     with ExitStack() as ctx:
         const = ctx.enter_context(tc.tile_pool(name="const", bufs=1))
         xin = ctx.enter_context(tc.tile_pool(name="xin", bufs=1))
-        junkv = ctx.enter_context(tc.tile_pool(name="junkv", bufs=8))
+        junkv = ctx.enter_context(tc.tile_pool(name="junkv", bufs=4))
         junks = ctx.enter_context(tc.tile_pool(name="junks", bufs=4))
         xcp = ctx.enter_context(tc.tile_pool(name="xcp", bufs=3))
-        grpp = ctx.enter_context(tc.tile_pool(name="grpp", bufs=4))
+        grpp = ctx.enter_context(tc.tile_pool(name="grpp", bufs=3))
         qp = ctx.enter_context(tc.tile_pool(name="qp", bufs=2))
-        outp = ctx.enter_context(tc.tile_pool(name="outp", bufs=4))
-        tpp = ctx.enter_context(tc.psum_pool(name="tpp", bufs=5))
+        outp = ctx.enter_context(tc.tile_pool(name="outp", bufs=3))
+        tpp = ctx.enter_context(tc.psum_pool(name="tpp", bufs=6))
         accp = ctx.enter_context(tc.psum_pool(name="accp", bufs=2))
-        foldp = ctx.enter_context(tc.psum_pool(name="foldp", bufs=1))
         ctx.enter_context(tc.manual_schedule())
 
         xg = {}
@@ -93,7 +89,7 @@ def tile_covpool_kernel(tc, x, out):
             return xg[b // GI][:, b % GI, :]
 
         def fold(b):
-            folded[b] = foldp.tile([P, P], F32, name="fold%d" % b, tag="fold")
+            folded[b] = tpp.tile([P, P], F32, name="fold%d" % b, tag="tp")
             for q in range(K // P):
                 nc.tensor.matmul(
                     out=folded[b][:],
@@ -103,9 +99,12 @@ def tile_covpool_kernel(tc, x, out):
                     stop=(q == K // P - 1),
                 )
 
+        def off_vector(b):
+            return is_folded(b) or on_scalar(b)
+
         def sum_of(b):
             negmean[b] = const.tile([P, 1], F32, name="nm%d" % b, tag="nm%d" % b)
-            if is_folded(b) or on_scalar(b):
+            if off_vector(b):
                 source = folded[b][:] if is_folded(b) else image(b)
                 n = P if is_folded(b) else K
                 js = junks.tile([P, K], BF16, name="js%d" % b, tag="js")
@@ -124,36 +123,45 @@ def tile_covpool_kernel(tc, x, out):
                     accum_out=negmean[b][:],
                 )
 
-        def subtract(u):
-            xc[u] = xcp.tile([P, UI, K], BF16, name="xc%d" % u, tag="xc")
-            for i in range(UI):
-                b = UI * u + i
-                nc.vector.tensor_scalar(
-                    out=xc[u][:, i, :],
+        def subtract(b):
+            g, i = divmod(b, GI)
+            if i == 0:
+                xc[g] = xcp.tile([P, GI, K], BF16, name="xc%d" % g, tag="xc")
+            if on_gpsimd(b):
+                nc.gpsimd.tensor_scalar(
+                    out=xc[g][:, i, :],
                     in0=image(b),
+                    scalar1=negmean[b][:],
+                    scalar2=1.0,
+                    op0=ALU.add,
+                    op1=ALU.mult,
+                )
+            else:
+                end = K * (i + 1) + (2 if on_gpsimd(b + 1) else 0)
+                nc.vector.tensor_scalar(
+                    out=xc[g][:].rearrange("p i k -> p (i k)")[:, K * i : end],
+                    in0=xg[g][:].rearrange("p i k -> p (i k)")[:, K * i : end],
                     scalar1=negmean[b][:],
                     scalar2=None,
                     op0=ALU.add,
                 )
 
-        def transpose(u):
-            for i in range(UI):
-                words = xc[u][:, i, :].bitcast(F32)
-                t = tpp.tile([P, 4, P], F32, name="tp%d_%d" % (u, i), tag="tp")
-                for q in range(4):
-                    nc.tensor.transpose(out=t[:, q, :], in_=words[:, P * q : P * q + P], identity=ident[:])
-                tp[UI * u + i] = t
+        def transpose(b):
+            g, i = divmod(b, GI)
+            words = xc[g][:, i, :].bitcast(F32)
+            tp[b] = tpp.tile([P, 4, P], F32, name="tp%d" % b, tag="tp")
+            for q in range(4):
+                nc.tensor.transpose(out=tp[b][:, q, :], in_=words[:, P * q : P * q + P], identity=ident[:])
 
-        def copy_out(u):
-            g = UI * u // GI
-            if UI * u % GI == 0:
+        def copy_out(b):
+            g, i = divmod(b, GI)
+            if i == 0:
                 grp[g] = grpp.tile([P, GI, K], BF16, name="grp%d" % g, tag="grp", align_bytes=64)
-            for i in reversed(range(UI)):
-                b = UI * u + i
-                nc.scalar.copy(
-                    out=grp[g][:, b % GI, :].bitcast(F32).rearrange("p (a c u) -> p a c u", a=2, u=2),
-                    in_=tp[b][:].rearrange("p (a u) c -> p a c u", a=2),
-                )
+            copy = nc.vector.tensor_copy if copied_by_vector(b) else nc.scalar.copy
+            copy(
+                out=grp[g][:, i, :].bitcast(F32).rearrange("p (a c u) -> p a c u", a=2, u=2),
+                in_=tp[b][:].rearrange("p (a u) c -> p a c u", a=2),
+            )
 
         def quantise(g, lo, hi):
             if lo == 0:
@@ -187,37 +195,39 @@ def tile_covpool_kernel(tc, x, out):
             nc.scalar.activation(out=ost[g][:, lo:hi, :], in_=acc[g][:, lo:hi, :], func=ACT.Copy, scale=1.0 / K)
             nc.sync.dma_start(out=ov[:, GI * g + lo : GI * g + hi, :], in_=ost[g][:, lo:hi, :])
 
-        def live(u):
-            return 0 <= u < NU
+        def live(g):
+            return 0 <= g < NG
 
-        def group_at(t, lag):
-            g, odd = divmod(t - lag, 2)
-            return g if odd == 0 and 0 <= g < NG else None
+        def images(g):
+            return range(GI * g, GI * g + GI) if live(g) else []
 
-        for t in range(-2, NU + 7):
-            if live(t + 1):
-                subtract(t + 1)
-            g = group_at(t, 3)
-            if g is not None:
-                for lo, hi in pieces(g):
-                    quantise(g, lo, hi)
-            if live(t):
-                transpose(t)
-            if live(t):
-                copy_out(t)
-            for b in range(B):
-                if is_folded(b) and fold_step(b) == t:
+        for b in images(0):
+            sum_of(b)
+            if b >= 1:
+                subtract(b - 1)
+        subtract(GI - 1)
+        for s in range(-1, NG + 3):
+            if s >= 0:
+                for b in images(s + 1):
+                    subtract(b)
+            for b in images(s):
+                transpose(b)
+            for b in images(s):
+                copy_out(b)
+            for b in images(s + 2):
+                if is_folded(b):
                     fold(b)
-            for b in range(B):
-                if sum_step(b) == t:
+            for b in images(s + 2):
+                if True:
                     sum_of(b)
-            g = group_at(t, 4)
-            if g is not None:
-                for lo, hi in pieces(g):
-                    multiply(g, lo, hi)
-            g = group_at(t, 5)
-            if g is not None:
-                for lo, hi in pieces(g):
-                    finish(g, lo, hi)
-                if g + AHEAD < NG:
-                    load(g + AHEAD)
+            if live(s - 1):
+                for lo, hi in pieces(s - 1):
+                    quantise(s - 1, lo, hi)
+            if live(s - 2):
+                for lo, hi in pieces(s - 2):
+                    multiply(s - 2, lo, hi)
+            if live(s - 2):
+                for lo, hi in pieces(s - 2):
+                    finish(s - 2, lo, hi)
+                if s - 2 + AHEAD < NG:
+                    load(s - 2 + AHEAD)

@@ -20,6 +20,7 @@ GI = 4
 NG = B // GI
 WORDS = 2 * P
 AHEAD = 8
+SUBTRACT_ORDER = (0, 2, 1, 3)
 
 
 def on_scalar(b):
@@ -27,7 +28,7 @@ def on_scalar(b):
 
 
 def is_folded(b):
-    return b % 12 == 11
+    return b % 10 == 3 and b > 3
 
 
 def on_gpsimd(b):
@@ -35,7 +36,7 @@ def on_gpsimd(b):
 
 
 def copied_by_vector(b):
-    return b == B - 1
+    return b == B - 3
 
 
 def pieces(g):
@@ -207,18 +208,22 @@ def tile_covpool_kernel(tc, x, out):
                 subtract(b - 1)
         subtract(GI - 1)
         for s in range(-1, NG + 3):
-            if s >= 0:
-                for b in images(s + 1):
-                    subtract(b)
             for b in images(s):
                 transpose(b)
             for b in images(s):
                 copy_out(b)
+                if b == 1:
+                    for later in images(1):
+                        if off_vector(later):
+                            sum_of(later)
+            if s >= 0:
+                for b in images(s + 1):
+                    subtract(GI * (s + 1) + SUBTRACT_ORDER[b % GI])
             for b in images(s + 2):
                 if is_folded(b):
                     fold(b)
             for b in images(s + 2):
-                if True:
+                if s >= 0 or not off_vector(b):
                     sum_of(b)
             if live(s - 1):
                 for lo, hi in pieces(s - 1):

from contextlib import ExitStack

import concourse.mybir as mybir
from concourse.masks import make_identity

FLOPS = 2 * 64 * 128 * 128 * 1024

BF16 = mybir.dt.bfloat16
F32 = mybir.dt.float32
U32 = mybir.dt.uint32
U8 = mybir.dt.uint8
FP8X4 = mybir.dt.float8_e4m3fn_x4
ALU = mybir.AluOpType
ACT = mybir.ActivationFunctionType

P = 128
B = 64
K = 1024
GI = 4
NG = B // GI
WORDS = 2 * P
AHEAD = 8
SUBTRACT_ORDER = (0, 2, 1, 3)


def on_scalar(b):
    return b % 4 == 3


def is_folded(b):
    return b % 10 == 3 and b > 3


def on_gpsimd(b):
    return b % 4 == 3 and 0 < b // GI < NG - 1


def copied_by_vector(b):
    return b == B - 3


def pieces(g):
    return [(0, 2), (2, 3), (3, 4)] if g == NG - 1 else [(0, GI)]


def tile_covpool_kernel(tc, x, out):
    nc = tc.nc
    xv = x.rearrange("b c y z -> c b (y z)")
    ov = out.rearrange("b c n -> c b n")

    with ExitStack() as ctx:
        const = ctx.enter_context(tc.tile_pool(name="const", bufs=1))
        xin = ctx.enter_context(tc.tile_pool(name="xin", bufs=1))
        junkv = ctx.enter_context(tc.tile_pool(name="junkv", bufs=4))
        junks = ctx.enter_context(tc.tile_pool(name="junks", bufs=4))
        xcp = ctx.enter_context(tc.tile_pool(name="xcp", bufs=3))
        grpp = ctx.enter_context(tc.tile_pool(name="grpp", bufs=3))
        qp = ctx.enter_context(tc.tile_pool(name="qp", bufs=2))
        outp = ctx.enter_context(tc.tile_pool(name="outp", bufs=3))
        tpp = ctx.enter_context(tc.psum_pool(name="tpp", bufs=6))
        accp = ctx.enter_context(tc.psum_pool(name="accp", bufs=2))
        ctx.enter_context(tc.manual_schedule())

        xg = {}
        xc = {}
        tp = {}
        grp = {}
        codes = {}
        scl = {}
        acc = {}
        ost = {}
        negmean = {}
        folded = {}

        def load(g):
            xg[g] = xin.tile([P, GI, K], BF16, name="x%d" % g, tag="x%d" % g)
            cuts = {0: [0, 1, 2, 4], 1: [0, 2, 4]}.get(g, [0, 4])
            for lo, hi in zip(cuts[:-1], cuts[1:]):
                nc.sync.dma_start(out=xg[g][:, lo:hi, :], in_=xv[:, GI * g + lo : GI * g + hi, :])

        for g in range(AHEAD):
            load(g)

        ident = const.tile([P, P], F32, name="ident")
        make_identity(nc, ident[:])
        ident16 = const.tile([P, P], BF16, name="ident16")
        nc.gpsimd.tensor_copy(out=ident16[:], in_=ident[:])

        def image(b):
            return xg[b // GI][:, b % GI, :]

        def fold(b):
            folded[b] = tpp.tile([P, P], F32, name="fold%d" % b, tag="tp")
            for q in range(K // P):
                nc.tensor.matmul(
                    out=folded[b][:],
                    lhsT=ident16[:],
                    rhs=image(b)[:, P * q : P * q + P],
                    start=(q == 0),
                    stop=(q == K // P - 1),
                )

        def off_vector(b):
            return is_folded(b) or on_scalar(b)

        def sum_of(b):
            negmean[b] = const.tile([P, 1], F32, name="nm%d" % b, tag="nm%d" % b)
            if off_vector(b):
                source = folded[b][:] if is_folded(b) else image(b)
                n = P if is_folded(b) else K
                js = junks.tile([P, K], BF16, name="js%d" % b, tag="js")
                nc.scalar.activation(
                    out=js[:, 0:n], in_=source, func=ACT.Copy, scale=-1.0 / K, accum_out=negmean[b][:]
                )
            else:
                jv = junkv.tile([P, K], BF16, name="jv%d" % b, tag="jv")
                nc.vector.tensor_scalar(
                    out=jv[:],
                    in0=image(b),
                    scalar1=-1.0 / K,
                    scalar2=None,
                    op0=ALU.mult,
                    op1=ALU.add,
                    accum_out=negmean[b][:],
                )

        def subtract(b):
            g, i = divmod(b, GI)
            if i == 0:
                xc[g] = xcp.tile([P, GI, K], BF16, name="xc%d" % g, tag="xc")
            if on_gpsimd(b):
                nc.gpsimd.tensor_scalar(
                    out=xc[g][:, i, :],
                    in0=image(b),
                    scalar1=negmean[b][:],
                    scalar2=1.0,
                    op0=ALU.add,
                    op1=ALU.mult,
                )
            else:
                end = K * (i + 1) + (2 if on_gpsimd(b + 1) else 0)
                nc.vector.tensor_scalar(
                    out=xc[g][:].rearrange("p i k -> p (i k)")[:, K * i : end],
                    in0=xg[g][:].rearrange("p i k -> p (i k)")[:, K * i : end],
                    scalar1=negmean[b][:],
                    scalar2=None,
                    op0=ALU.add,
                )

        def transpose(b):
            g, i = divmod(b, GI)
            words = xc[g][:, i, :].bitcast(F32)
            tp[b] = tpp.tile([P, 4, P], F32, name="tp%d" % b, tag="tp")
            for q in range(4):
                nc.tensor.transpose(out=tp[b][:, q, :], in_=words[:, P * q : P * q + P], identity=ident[:])

        def copy_out(b):
            g, i = divmod(b, GI)
            if i == 0:
                grp[g] = grpp.tile([P, GI, K], BF16, name="grp%d" % g, tag="grp", align_bytes=64)
            copy = nc.vector.tensor_copy if copied_by_vector(b) else nc.scalar.copy
            copy(
                out=grp[g][:, i, :].bitcast(F32).rearrange("p (a c u) -> p a c u", a=2, u=2),
                in_=tp[b][:].rearrange("p (a u) c -> p a c u", a=2),
            )

        def quantise(g, lo, hi):
            if lo == 0:
                codes[g] = qp.tile([P, GI * WORDS], U32, name="codes%d" % g, tag="codes", align_bytes=64)
                scl[g] = qp.tile([P, GI * WORDS], U8, name="scl%d" % g, tag="scl", align_bytes=64)
            nc.vector.quantize_mx(
                out=codes[g][:, WORDS * lo : WORDS * hi].bitcast(FP8X4),
                scales=scl[g][:, WORDS * lo : WORDS * hi],
                in_=grp[g][:, lo:hi, :].rearrange("p i w -> p (i w)"),
            )

        def multiply(g, lo, hi):
            if lo == 0:
                acc[g] = accp.tile([P, GI, P], F32, name="acc%d" % g, tag="acc")
            for i in range(lo, hi):
                for a in range(2):
                    off = WORDS * i + P * a
                    nc.tensor.matmul_mx(
                        out=acc[g][:, i, :],
                        lhsT=codes[g][:, off : off + P].bitcast(FP8X4),
                        lhsT_scale=scl[g][:, off : off + P],
                        rhs=codes[g][:, off : off + P].bitcast(FP8X4),
                        rhs_scale=scl[g][:, off : off + P],
                        start=(a == 0),
                        stop=(a == 1),
                    )

        def finish(g, lo, hi):
            if lo == 0:
                ost[g] = outp.tile([P, GI, P], F32, name="ost%d" % g, tag="ost")
            nc.scalar.activation(out=ost[g][:, lo:hi, :], in_=acc[g][:, lo:hi, :], func=ACT.Copy, scale=1.0 / K)
            nc.sync.dma_start(out=ov[:, GI * g + lo : GI * g + hi, :], in_=ost[g][:, lo:hi, :])

        def live(g):
            return 0 <= g < NG

        def images(g):
            return range(GI * g, GI * g + GI) if live(g) else []

        for b in images(0):
            sum_of(b)
            if b >= 1:
                subtract(b - 1)
        subtract(GI - 1)
        for s in range(-1, NG + 3):
            for b in images(s):
                transpose(b)
            for b in images(s):
                copy_out(b)
                if b == 1:
                    for later in images(1):
                        if off_vector(later):
                            sum_of(later)
            if s >= 0:
                for b in images(s + 1):
                    subtract(GI * (s + 1) + SUBTRACT_ORDER[b % GI])
            for b in images(s + 2):
                if is_folded(b):
                    fold(b)
            for b in images(s + 2):
                if s >= 0 or not off_vector(b):
                    sum_of(b)
            if live(s - 1):
                for lo, hi in pieces(s - 1):
                    quantise(s - 1, lo, hi)
            if live(s - 2):
                for lo, hi in pieces(s - 2):
                    multiply(s - 2, lo, hi)
            if live(s - 2):
                for lo, hi in pieces(s - 2):
                    finish(s - 2, lo, hi)
                if s - 2 + AHEAD < NG:
                    load(s - 2 + AHEAD)
